import numpy as np
import ml_dtypes

BF16 = ml_dtypes.bfloat16


def bf(x):
    return np.asarray(x, np.float32).astype(BF16)


def f32(x):
    return np.asarray(x, np.float32)


def f64(x):
    return np.asarray(x).astype(np.float64)


def striped(idx):
    return np.tile(idx.reshape(-1, 16).T, (8, 1))


S, D, H, M, B, T, N = 2048, 128, 128, 256, 64, 64, 4096


def setup_inputs():
    table = bf(np.random.standard_normal((D, S)))
    w_att = 1.5 * np.random.standard_normal((D, H)) / np.sqrt(D)
    w_mlp = 3.0 * np.random.standard_normal((D, M - H)) / np.sqrt(D)
    return {"table": table, "w": bf(np.concatenate([w_att, w_mlp], axis=1)), "b1": f32(0.2 * np.random.standard_normal((H, 1))), "w2": bf(2.0 * np.random.standard_normal((H, 1)) / np.sqrt(H)), "bm": f32(0.2 * np.random.standard_normal((M - H, 1))), "offs": striped(np.random.permutation(np.tile(np.arange(S), 2))[:N])}


def reference(table, w, b1, w2, bm, offs):
    idx = offs[:16].T.reshape(-1)
    y = f64(w).T @ f64(table)[:, idx]
    dec = 1.0 - np.arange(T) / T
    h = np.tanh(y[:H] * np.tile(dec, B)[None, :] + f64(b1))
    score = (f64(w2).T @ h).reshape(B, T)
    e = np.exp(score - score.max(axis=1, keepdims=True))
    alpha = e / e.sum(axis=1, keepdims=True)
    coef = alpha * dec[None, :] + 1.0 / T
    pooled = (y[H:].reshape(M - H, B, T) * coef[None, :, :]).sum(axis=2)
    return np.tanh(pooled + f64(bm))

@@ -1,0 +1,188 @@
+import concourse.mybir as mybir
+
+F32 = mybir.dt.float32
+BF16 = mybir.dt.bfloat16
+U16 = mybir.dt.uint16
+I32 = mybir.dt.int32
+ALU = mybir.AluOpType
+ACT = mybir.ActivationFunctionType
+AXIS = mybir.AxisListType
+
+P = 128
+WORDS = 2048
+ENTRIES = 4096
+T = 64
+SENTENCES = ENTRIES // T
+PIECE = 512
+PER_PIECE = PIECE // T
+GROUP = 32
+GROUPS = SENTENCES // GROUP
+PIECES_PER_GROUP = GROUP // PER_PIECE
+
+FLOPS = 2 * P * (2 * P) * ENTRIES + 2 * P * ENTRIES
+
+
+def tile_cabasc_kernel(tc, table, w, b1, w2, bm, offs, out):
+    nc = tc.nc
+    with (
+        tc.tile_pool(name="held", bufs=1) as held,
+        tc.tile_pool(name="work", bufs=3) as work,
+        tc.tile_pool(name="small", bufs=2) as small,
+        tc.psum_pool(name="psum", bufs=1) as psum,
+    ):
+        offsets = held.tile([P, ENTRIES // 16], U16, name="offsets")
+        nc.sync.dma_start(offsets[:], offs)
+        window = held.tile([P, WORDS], BF16, name="window")
+        nc.sync.dma_start(window[:], table)
+        weights = held.tile([P, 2 * P], BF16, name="weights")
+        nc.scalar.dma_start(weights[:], w)
+        w2_column = held.tile([P, 1], BF16, name="w2_column")
+        nc.scalar.dma_start(w2_column[:], w2)
+        b1_column = held.tile([P, 1], F32, name="b1_column")
+        nc.scalar.dma_start(b1_column[:], b1)
+        bm_column = held.tile([P, 1], F32, name="bm_column")
+        nc.scalar.dma_start(bm_column[:], bm)
+
+        position = held.tile([P, PIECE], I32, name="position")
+        nc.gpsimd.iota(position[:], pattern=[[0, PER_PIECE], [1, T]], base=0, channel_multiplier=0)
+        dec = held.tile([P, PIECE], F32, name="dec")
+        nc.vector.tensor_scalar(dec[:], position[:], -1.0 / T, 1.0, ALU.mult, ALU.add)
+
+        w2_spread = held.tile([P, P + GROUP], BF16, name="w2_spread")
+        nc.vector.memset(w2_spread[:], 0.0)
+        nc.vector.tensor_copy(
+            w2_spread[:].rearrange("p (c s) -> p c s", s=GROUP)[:, :, GROUP - 1 : GROUP],
+            w2_column[:, 0:1].unsqueeze(2).to_broadcast([P, (P + GROUP) // GROUP, 1]),
+        )
+
+        pick = held.tile([P, GROUP], BF16, name="pick")
+        nc.gpsimd.memset(pick[:], 0.0)
+        for copy in range(3):
+            nc.gpsimd.affine_select(
+                out=pick[:],
+                in_=pick[:],
+                compare_op=ALU.not_equal,
+                fill=1.0,
+                base=-copy * GROUP,
+                pattern=[[-1, GROUP]],
+                channel_multiplier=1,
+            )
+
+        from_copy_1 = held.tile([P, 1], F32, name="from_copy_1")
+        nc.vector.memset(from_copy_1[:], -1.0)
+        nc.vector.memset(from_copy_1[0:GROUP], 0.0)
+        from_copy_2 = held.tile([P, 1], F32, name="from_copy_2")
+        nc.vector.memset(from_copy_2[:], -1.0)
+        nc.vector.memset(from_copy_2[0 : 2 * GROUP], 0.0)
+
+        hidden = held.tile([P, ENTRIES], BF16, name="hidden")
+        y_mlp = held.tile([P, ENTRIES], F32, name="y_mlp")
+        pooled = held.tile([P, SENTENCES], F32, name="pooled")
+
+        def looked_up(piece):
+            return window[:].indirect(offsets[:, piece * (PIECE // 16) : (piece + 1) * (PIECE // 16)])
+
+        def attention_hidden(piece):
+            y_att = psum.tile([P, PIECE], F32, name="y_att", tag="bank", bufs=4)
+            nc.tensor.matmul(y_att[:], weights[:, 0:P], looked_up(piece), start=True, stop=True)
+            weighted = work.tile([P, PIECE], F32, name="weighted")
+            nc.vector.tensor_tensor(weighted[:], y_att[:], dec[:], ALU.mult)
+            nc.scalar.activation(
+                hidden[:, piece * PIECE : (piece + 1) * PIECE],
+                weighted[:],
+                ACT.Tanh,
+                bias=b1_column[:, 0:1],
+                scale=1.0,
+            )
+
+        def pooling_weights(group):
+            score = psum.tile([P, T], F32, name="score", tag="bank", bufs=4)
+            for s in reversed(range(GROUP)):
+                first = (group * GROUP + s) * T
+                nc.tensor.matmul(
+                    score[:],
+                    w2_spread[:, GROUP - 1 - s : GROUP - 1 - s + P],
+                    hidden[:, first : first + T],
+                    start=(s == GROUP - 1),
+                    stop=(s == 0),
+                )
+            neg_max = small.tile([P, 1], F32, name="neg_max")
+            nc.vector.tensor_reduce(neg_max[:], score[:], AXIS.X, ALU.max, negate=True)
+            expd = small.tile([P, T], F32, name="expd")
+            exp_sum = small.tile([P, 1], F32, name="exp_sum")
+            nc.scalar.activation(
+                expd[:], score[:], ACT.Exp, bias=neg_max[:, 0:1], scale=1.0, accum_out=exp_sum[:, 0:1]
+            )
+            inverse = small.tile([P, 1], F32, name="inverse")
+            nc.vector.reciprocal(inverse[:], exp_sum[:])
+            attended = small.tile([P, T], F32, name="attended")
+            nc.vector.scalar_tensor_tensor(
+                attended[:], expd[:], inverse[:, 0:1], dec[:, 0:T], ALU.mult, ALU.mult
+            )
+            term_1 = small.tile([P, T], BF16, name="term_1")
+            nc.vector.tensor_copy(term_1[:], attended[:])
+            rest = small.tile([P, T], F32, name="rest")
+            nc.vector.scalar_tensor_tensor(
+                rest[:], term_1[:], from_copy_1[:, 0:1], attended[:], ALU.mult, ALU.add
+            )
+            term_2 = small.tile([P, T], BF16, name="term_2")
+            nc.vector.tensor_copy(term_2[:], rest[:])
+            terms = small.tile([P, T], BF16, name="terms")
+            nc.vector.scalar_tensor_tensor(
+                terms[:], term_2[:], from_copy_2[:, 0:1], rest[:], ALU.mult, ALU.add
+            )
+            return terms
+
+        def project_output(piece):
+            y_bank = psum.tile([P, PIECE], F32, name="y_bank", tag="bank", bufs=4)
+            nc.tensor.matmul(y_bank[:], weights[:, P : 2 * P], looked_up(piece), start=True, stop=True)
+            nc.scalar.copy(y_mlp[:, piece * PIECE : (piece + 1) * PIECE], y_bank[:])
+
+        def repeat_weights(terms):
+            repeated = psum.tile([P, GROUP * T], F32, name="repeated")
+            for s in range(GROUP):
+                nc.tensor.matmul(
+                    repeated[:, s * T : (s + 1) * T],
+                    pick[:, s : s + 1].to_broadcast([P, P]),
+                    terms[:],
+                    start=True,
+                    stop=True,
+                )
+            return repeated
+
+        def pool_group(group, repeated):
+            for i in range(PIECES_PER_GROUP):
+                piece = group * PIECES_PER_GROUP + i
+                product = work.tile([P, PIECE], F32, name="product")
+                nc.vector.scalar_tensor_tensor(
+                    product[:],
+                    repeated[:, i * PIECE : (i + 1) * PIECE],
+                    1.0 / T,
+                    y_mlp[:, piece * PIECE : (piece + 1) * PIECE],
+                    ALU.add,
+                    ALU.mult,
+                )
+                nc.vector.tensor_reduce(
+                    pooled[:, piece * PER_PIECE : (piece + 1) * PER_PIECE],
+                    product[:].rearrange("p (n t) -> p n t", t=T),
+                    AXIS.X,
+                    ALU.add,
+                )
+
+        for i in range(PIECES_PER_GROUP):
+            attention_hidden(i)
+        repeated_0 = repeat_weights(pooling_weights(0))
+        for i in range(PIECES_PER_GROUP):
+            attention_hidden(PIECES_PER_GROUP + i)
+        terms_1 = pooling_weights(1)
+        for i in range(PIECES_PER_GROUP):
+            project_output(i)
+        pool_group(0, repeated_0)
+        repeated_1 = repeat_weights(terms_1)
+        for i in range(PIECES_PER_GROUP):
+            project_output(PIECES_PER_GROUP + i)
+        pool_group(1, repeated_1)
+
+        result = held.tile([P, SENTENCES], F32, name="result")
+        nc.scalar.activation(result[:], pooled[:], ACT.Tanh, bias=bm_column[:, 0:1], scale=1.0)
+        nc.sync.dma_start(out, result[:])

@@ -76,14 +76,14 @@ def tile_cabasc_kernel(tc, table, w, b1, w2, bm, offs, out):
         nc.vector.memset(from_copy_2[0 : 2 * GROUP], 0.0)
 
         hidden = held.tile([P, ENTRIES], BF16, name="hidden")
-        y_mlp = held.tile([P, ENTRIES], F32, name="y_mlp")
+        coef = held.tile([P, ENTRIES], F32, name="coef")
         pooled = held.tile([P, SENTENCES], F32, name="pooled")
 
         def looked_up(piece):
             return window[:].indirect(offsets[:, piece * (PIECE // 16) : (piece + 1) * (PIECE // 16)])
 
         def attention_hidden(piece):
-            y_att = psum.tile([P, PIECE], F32, name="y_att", tag="bank", bufs=4)
+            y_att = psum.tile([P, PIECE], F32, name="y_att", tag="y", bufs=3)
             nc.tensor.matmul(y_att[:], weights[:, 0:P], looked_up(piece), start=True, stop=True)
             weighted = work.tile([P, PIECE], F32, name="weighted")
             nc.vector.tensor_tensor(weighted[:], y_att[:], dec[:], ALU.mult)
@@ -96,7 +96,7 @@ def tile_cabasc_kernel(tc, table, w, b1, w2, bm, offs, out):
             )
 
         def pooling_weights(group):
-            score = psum.tile([P, T], F32, name="score", tag="bank", bufs=4)
+            score = psum.tile([P, T], F32, name="score")
             for s in reversed(range(GROUP)):
                 first = (group * GROUP + s) * T
                 nc.tensor.matmul(
@@ -115,30 +115,27 @@ def tile_cabasc_kernel(tc, table, w, b1, w2, bm, offs, out):
             )
             inverse = small.tile([P, 1], F32, name="inverse")
             nc.vector.reciprocal(inverse[:], exp_sum[:])
-            attended = small.tile([P, T], F32, name="attended")
-            nc.vector.scalar_tensor_tensor(
-                attended[:], expd[:], inverse[:, 0:1], dec[:, 0:T], ALU.mult, ALU.mult
-            )
-            term_1 = small.tile([P, T], BF16, name="term_1")
-            nc.vector.tensor_copy(term_1[:], attended[:])
+            decayed = small.tile([P, T], F32, name="decayed")
+            nc.vector.tensor_tensor(decayed[:], expd[:], dec[:, 0:T], ALU.mult)
+            value = small.tile([P, T], F32, name="value")
+            nc.vector.tensor_scalar(value[:], decayed[:], inverse[:, 0:1], 1.0 / T, ALU.mult, ALU.add)
+            value_16 = small.tile([P, T], BF16, name="value_16")
+            nc.vector.tensor_scalar(value_16[:], decayed[:], inverse[:, 0:1], 1.0 / T, ALU.mult, ALU.add)
             rest = small.tile([P, T], F32, name="rest")
             nc.vector.scalar_tensor_tensor(
-                rest[:], term_1[:], from_copy_1[:, 0:1], attended[:], ALU.mult, ALU.add
+                rest[:], value_16[:], from_copy_1[:, 0:1], value[:], ALU.mult, ALU.add
             )
-            term_2 = small.tile([P, T], BF16, name="term_2")
-            nc.vector.tensor_copy(term_2[:], rest[:])
+            rest_16 = small.tile([P, T], BF16, name="rest_16")
+            nc.vector.scalar_tensor_tensor(
+                rest_16[:], value_16[:], from_copy_1[:, 0:1], value[:], ALU.mult, ALU.add
+            )
             terms = small.tile([P, T], BF16, name="terms")
             nc.vector.scalar_tensor_tensor(
-                terms[:], term_2[:], from_copy_2[:, 0:1], rest[:], ALU.mult, ALU.add
+                terms[:], rest_16[:], from_copy_2[:, 0:1], rest[:], ALU.mult, ALU.add
             )
             return terms
 
-        def project_output(piece):
-            y_bank = psum.tile([P, PIECE], F32, name="y_bank", tag="bank", bufs=4)
-            nc.tensor.matmul(y_bank[:], weights[:, P : 2 * P], looked_up(piece), start=True, stop=True)
-            nc.scalar.copy(y_mlp[:, piece * PIECE : (piece + 1) * PIECE], y_bank[:])
-
-        def repeat_weights(terms):
+        def repeat_weights(group, terms):
             repeated = psum.tile([P, GROUP * T], F32, name="repeated")
             for s in range(GROUP):
                 nc.tensor.matmul(
@@ -148,40 +145,28 @@ def tile_cabasc_kernel(tc, table, w, b1, w2, bm, offs, out):
                     start=True,
                     stop=True,
                 )
-            return repeated
-
-        def pool_group(group, repeated):
             for i in range(PIECES_PER_GROUP):
-                piece = group * PIECES_PER_GROUP + i
-                product = work.tile([P, PIECE], F32, name="product")
-                nc.vector.scalar_tensor_tensor(
-                    product[:],
-                    repeated[:, i * PIECE : (i + 1) * PIECE],
-                    1.0 / T,
-                    y_mlp[:, piece * PIECE : (piece + 1) * PIECE],
-                    ALU.add,
-                    ALU.mult,
-                )
-                nc.vector.tensor_reduce(
-                    pooled[:, piece * PER_PIECE : (piece + 1) * PER_PIECE],
-                    product[:].rearrange("p (n t) -> p n t", t=T),
-                    AXIS.X,
-                    ALU.add,
-                )
+                first = (group * PIECES_PER_GROUP + i) * PIECE
+                nc.scalar.copy(coef[:, first : first + PIECE], repeated[:, i * PIECE : (i + 1) * PIECE])
 
-        for i in range(PIECES_PER_GROUP):
-            attention_hidden(i)
-        repeated_0 = repeat_weights(pooling_weights(0))
-        for i in range(PIECES_PER_GROUP):
-            attention_hidden(PIECES_PER_GROUP + i)
-        terms_1 = pooling_weights(1)
-        for i in range(PIECES_PER_GROUP):
-            project_output(i)
-        pool_group(0, repeated_0)
-        repeated_1 = repeat_weights(terms_1)
-        for i in range(PIECES_PER_GROUP):
-            project_output(PIECES_PER_GROUP + i)
-        pool_group(1, repeated_1)
+        def pool(piece):
+            y_mlp = psum.tile([P, PIECE], F32, name="y_mlp", tag="y", bufs=3)
+            nc.tensor.matmul(y_mlp[:], weights[:, P : 2 * P], looked_up(piece), start=True, stop=True)
+            product = work.tile([P, PIECE], F32, name="product")
+            nc.vector.tensor_tensor(product[:], y_mlp[:], coef[:, piece * PIECE : (piece + 1) * PIECE], ALU.mult)
+            nc.vector.tensor_reduce(
+                pooled[:, piece * PER_PIECE : (piece + 1) * PER_PIECE],
+                product[:].rearrange("p (n t) -> p n t", t=T),
+                AXIS.X,
+                ALU.add,
+            )
+
+        for group in range(GROUPS):
+            for i in range(PIECES_PER_GROUP):
+                attention_hidden(group * PIECES_PER_GROUP + i)
+            repeat_weights(group, pooling_weights(group))
+        for piece in range(GROUPS * PIECES_PER_GROUP):
+            pool(piece)
 
         result = held.tile([P, SENTENCES], F32, name="result")
         nc.scalar.activation(result[:], pooled[:], ACT.Tanh, bias=bm_column[:, 0:1], scale=1.0)

@@ -30,18 +30,22 @@ def tile_cabasc_kernel(tc, table, w, b1, w2, bm, offs, out):
         tc.tile_pool(name="small", bufs=2) as small,
         tc.psum_pool(name="psum", bufs=1) as psum,
     ):
+        window = held.tile([P, WORDS], BF16, name="window")
+        nc.scalar.dma_start(window[:], table)
         offsets = held.tile([P, ENTRIES // 16], U16, name="offsets")
         nc.sync.dma_start(offsets[:], offs)
-        window = held.tile([P, WORDS], BF16, name="window")
-        nc.sync.dma_start(window[:], table)
         weights = held.tile([P, 2 * P], BF16, name="weights")
-        nc.scalar.dma_start(weights[:], w)
-        w2_column = held.tile([P, 1], BF16, name="w2_column")
-        nc.scalar.dma_start(w2_column[:], w2)
+        nc.sync.dma_start(weights[:], w)
         b1_column = held.tile([P, 1], F32, name="b1_column")
-        nc.scalar.dma_start(b1_column[:], b1)
+        nc.sync.dma_start(b1_column[:], b1)
+        w2_column = held.tile([P, 1], BF16, name="w2_column")
+        nc.sync.dma_start(w2_column[:], w2)
         bm_column = held.tile([P, 1], F32, name="bm_column")
-        nc.scalar.dma_start(bm_column[:], bm)
+        nc.sync.dma_start(bm_column[:], bm)
+
+        scratch = held.tile([P, 1], F32, name="scratch")
+        nc.vector.memset(scratch[:], 0.0)
+        nc.scalar.activation(scratch[:], scratch[:], ACT.Tanh)
 
         position = held.tile([P, PIECE], I32, name="position")
         nc.gpsimd.iota(position[:], pattern=[[0, PER_PIECE], [1, T]], base=0, channel_multiplier=0)
@@ -135,23 +139,34 @@ def tile_cabasc_kernel(tc, table, w, b1, w2, bm, offs, out):
             )
             return terms
 
-        def repeat_weights(group, terms):
-            repeated = psum.tile([P, GROUP * T], F32, name="repeated")
-            for s in range(GROUP):
-                nc.tensor.matmul(
-                    repeated[:, s * T : (s + 1) * T],
-                    pick[:, s : s + 1].to_broadcast([P, P]),
-                    terms[:],
-                    start=True,
-                    stop=True,
-                )
-            for i in range(PIECES_PER_GROUP):
-                first = (group * PIECES_PER_GROUP + i) * PIECE
-                nc.scalar.copy(coef[:, first : first + PIECE], repeated[:, i * PIECE : (i + 1) * PIECE])
+        def banks_in_turn(group):
+            return list(range(PIECES_PER_GROUP)) if group % 2 == 0 else list(reversed(range(PIECES_PER_GROUP)))
 
-        def pool(piece):
+        def repeat_weights(group, terms):
+            repeated = [
+                psum.tile([P, PIECE], F32, name=f"repeated{i}", tag="repeated", bufs=PIECES_PER_GROUP)
+                for i in range(PIECES_PER_GROUP)
+            ]
+            for i in banks_in_turn(group):
+                for n in range(PER_PIECE):
+                    s = i * PER_PIECE + n
+                    nc.tensor.matmul(
+                        repeated[i][:, n * T : (n + 1) * T],
+                        pick[:, s : s + 1].to_broadcast([P, P]),
+                        terms[:],
+                        start=True,
+                        stop=True,
+                    )
+            for i in banks_in_turn(group):
+                first = (group * PIECES_PER_GROUP + i) * PIECE
+                nc.scalar.copy(coef[:, first : first + PIECE], repeated[i][:])
+
+        def project_output(piece):
             y_mlp = psum.tile([P, PIECE], F32, name="y_mlp", tag="y", bufs=3)
             nc.tensor.matmul(y_mlp[:], weights[:, P : 2 * P], looked_up(piece), start=True, stop=True)
+            return y_mlp
+
+        def pool(piece, y_mlp):
             product = work.tile([P, PIECE], F32, name="product")
             nc.vector.tensor_tensor(product[:], y_mlp[:], coef[:, piece * PIECE : (piece + 1) * PIECE], ALU.mult)
             nc.vector.tensor_reduce(
@@ -161,13 +176,22 @@ def tile_cabasc_kernel(tc, table, w, b1, w2, bm, offs, out):
                 ALU.add,
             )
 
-        for group in range(GROUPS):
-            for i in range(PIECES_PER_GROUP):
-                attention_hidden(group * PIECES_PER_GROUP + i)
-            repeat_weights(group, pooling_weights(group))
-        for piece in range(GROUPS * PIECES_PER_GROUP):
-            pool(piece)
+        turn = [group * PIECES_PER_GROUP + i for group in range(GROUPS) for i in banks_in_turn(group)]
+        ahead = 3
+        for i in range(PIECES_PER_GROUP):
+            attention_hidden(i)
+        terms_0 = pooling_weights(0)
+        for i in range(PIECES_PER_GROUP):
+            attention_hidden(PIECES_PER_GROUP + i)
+        waiting = [project_output(piece) for piece in turn[:ahead]]
+        terms_1 = pooling_weights(1)
+        repeat_weights(0, terms_0)
+        repeat_weights(1, terms_1)
+        for k, piece in enumerate(turn):
+            pool(piece, waiting[k])
+            if k + ahead < len(turn):
+                waiting.append(project_output(turn[k + ahead]))
 
         result = held.tile([P, SENTENCES], F32, name="result")
         nc.scalar.activation(result[:], pooled[:], ACT.Tanh, bias=bm_column[:, 0:1], scale=1.0)
-        nc.sync.dma_start(out, result[:])
+        nc.scalar.dma_start(out, result[:])

@@ -18,6 +18,7 @@ PER_PIECE = PIECE // T
 GROUP = 32
 GROUPS = SENTENCES // GROUP
 PIECES_PER_GROUP = GROUP // PER_PIECE
+VECTOR_SUMS = 5
 
 FLOPS = 2 * P * (2 * P) * ENTRIES + 2 * P * ENTRIES
 
@@ -169,12 +170,18 @@ def tile_cabasc_kernel(tc, table, w, b1, w2, bm, offs, out):
         def pool(piece, y_mlp):
             product = work.tile([P, PIECE], F32, name="product")
             nc.vector.tensor_tensor(product[:], y_mlp[:], coef[:, piece * PIECE : (piece + 1) * PIECE], ALU.mult)
+            first = piece * PER_PIECE
             nc.vector.tensor_reduce(
-                pooled[:, piece * PER_PIECE : (piece + 1) * PER_PIECE],
-                product[:].rearrange("p (n t) -> p n t", t=T),
+                pooled[:, first : first + VECTOR_SUMS],
+                product[:, 0 : VECTOR_SUMS * T].rearrange("p (n t) -> p n t", t=T),
                 AXIS.X,
                 ALU.add,
             )
+            for n in range(VECTOR_SUMS, PER_PIECE):
+                copied = work.tile([P, T], F32, name="copied")
+                nc.scalar.activation(
+                    copied[:], product[:, n * T : (n + 1) * T], ACT.Copy, accum_out=pooled[:, first + n : first + n + 1]
+                )
 
         turn = [group * PIECES_PER_GROUP + i for group in range(GROUPS) for i in banks_in_turn(group)]
         ahead = 3

@@ -160,7 +160,7 @@ def tile_cabasc_kernel(tc, table, w, b1, w2, bm, offs, out):
                     )
             for i in banks_in_turn(group):
                 first = (group * PIECES_PER_GROUP + i) * PIECE
-                nc.scalar.copy(coef[:, first : first + PIECE], repeated[i][:])
+                nc.any.tensor_copy(coef[:, first : first + PIECE], repeated[i][:])
 
         def project_output(piece):
             y_mlp = psum.tile([P, PIECE], F32, name="y_mlp", tag="y", bufs=3)

@@ -27,7 +27,7 @@ def tile_cabasc_kernel(tc, table, w, b1, w2, bm, offs, out):
     nc = tc.nc
     with (
         tc.tile_pool(name="held", bufs=1) as held,
-        tc.tile_pool(name="work", bufs=3) as work,
+        tc.tile_pool(name="work", bufs=6) as work,
         tc.tile_pool(name="small", bufs=2) as small,
         tc.psum_pool(name="psum", bufs=1) as psum,
     ):

@@ -84,6 +84,9 @@ def tile_cabasc_kernel(tc, table, w, b1, w2, bm, offs, out):
         coef = held.tile([P, ENTRIES], F32, name="coef")
         pooled = held.tile([P, SENTENCES], F32, name="pooled")
 
+        def upper_half(tile):
+            return tile[:].bitcast(BF16)[:, 1::2]
+
         def looked_up(piece):
             return window[:].indirect(offsets[:, piece * (PIECE // 16) : (piece + 1) * (PIECE // 16)])
 
@@ -120,56 +123,55 @@ def tile_cabasc_kernel(tc, table, w, b1, w2, bm, offs, out):
             )
             inverse = small.tile([P, 1], F32, name="inverse")
             nc.vector.reciprocal(inverse[:], exp_sum[:])
-            decayed = small.tile([P, T], F32, name="decayed")
-            nc.vector.tensor_tensor(decayed[:], expd[:], dec[:, 0:T], ALU.mult)
             value = small.tile([P, T], F32, name="value")
-            nc.vector.tensor_scalar(value[:], decayed[:], inverse[:, 0:1], 1.0 / T, ALU.mult, ALU.add)
-            value_16 = small.tile([P, T], BF16, name="value_16")
-            nc.vector.tensor_scalar(value_16[:], decayed[:], inverse[:, 0:1], 1.0 / T, ALU.mult, ALU.add)
+            nc.vector.scalar_tensor_tensor(
+                value[:], expd[:], inverse[:, 0:1], dec[:, 0:T], ALU.mult, ALU.mult
+            )
             rest = small.tile([P, T], F32, name="rest")
             nc.vector.scalar_tensor_tensor(
-                rest[:], value_16[:], from_copy_1[:, 0:1], value[:], ALU.mult, ALU.add
+                rest[:], upper_half(value), from_copy_1[:, 0:1], value[:], ALU.mult, ALU.add
             )
-            rest_16 = small.tile([P, T], BF16, name="rest_16")
+            terms = small.tile([P, T], F32, name="terms")
             nc.vector.scalar_tensor_tensor(
-                rest_16[:], value_16[:], from_copy_1[:, 0:1], value[:], ALU.mult, ALU.add
+                terms[:], upper_half(rest), from_copy_2[:, 0:1], rest[:], ALU.mult, ALU.add
             )
-            terms = small.tile([P, T], BF16, name="terms")
-            nc.vector.scalar_tensor_tensor(
-                terms[:], rest_16[:], from_copy_2[:, 0:1], rest[:], ALU.mult, ALU.add
-            )
-            return terms
-
-        def banks_in_turn(group):
-            return list(range(PIECES_PER_GROUP)) if group % 2 == 0 else list(reversed(range(PIECES_PER_GROUP)))
+            return upper_half(terms)
 
         def repeat_weights(group, terms):
-            repeated = [
-                psum.tile([P, PIECE], F32, name=f"repeated{i}", tag="repeated", bufs=PIECES_PER_GROUP)
-                for i in range(PIECES_PER_GROUP)
-            ]
-            for i in banks_in_turn(group):
+            repeated = []
+            for i in range(PIECES_PER_GROUP):
+                in_y_ring = group == 0 and i < 2
+                bank = psum.tile(
+                    [P, PIECE], F32, name=f"repeated{i}", tag="y" if in_y_ring else "repeated", bufs=3 if in_y_ring else 4
+                )
+                repeated.append(bank)
+            for i in range(PIECES_PER_GROUP):
                 for n in range(PER_PIECE):
                     s = i * PER_PIECE + n
                     nc.tensor.matmul(
                         repeated[i][:, n * T : (n + 1) * T],
                         pick[:, s : s + 1].to_broadcast([P, P]),
-                        terms[:],
+                        terms,
                         start=True,
                         stop=True,
                     )
-            for i in banks_in_turn(group):
+            for i in range(PIECES_PER_GROUP):
                 first = (group * PIECES_PER_GROUP + i) * PIECE
-                nc.any.tensor_copy(coef[:, first : first + PIECE], repeated[i][:])
+                nc.scalar.copy(coef[:, first : first + PIECE], repeated[i][:])
 
         def project_output(piece):
-            y_mlp = psum.tile([P, PIECE], F32, name="y_mlp", tag="y", bufs=3)
+            in_score_bank = piece == 1
+            y_mlp = psum.tile(
+                [P, PIECE], F32, name="y_mlp", tag="score" if in_score_bank else "y", bufs=1 if in_score_bank else 3
+            )
             nc.tensor.matmul(y_mlp[:], weights[:, P : 2 * P], looked_up(piece), start=True, stop=True)
             return y_mlp
 
         def pool(piece, y_mlp):
             product = work.tile([P, PIECE], F32, name="product")
-            nc.vector.tensor_tensor(product[:], y_mlp[:], coef[:, piece * PIECE : (piece + 1) * PIECE], ALU.mult)
+            nc.vector.scalar_tensor_tensor(
+                product[:], coef[:, piece * PIECE : (piece + 1) * PIECE], 1.0 / T, y_mlp[:], ALU.add, ALU.mult
+            )
             first = piece * PER_PIECE
             nc.vector.tensor_reduce(
                 pooled[:, first : first + VECTOR_SUMS],
@@ -183,21 +185,18 @@ def tile_cabasc_kernel(tc, table, w, b1, w2, bm, offs, out):
                     copied[:], product[:, n * T : (n + 1) * T], ACT.Copy, accum_out=pooled[:, first + n : first + n + 1]
                 )
 
-        turn = [group * PIECES_PER_GROUP + i for group in range(GROUPS) for i in banks_in_turn(group)]
-        ahead = 3
         for i in range(PIECES_PER_GROUP):
             attention_hidden(i)
         terms_0 = pooling_weights(0)
         for i in range(PIECES_PER_GROUP):
             attention_hidden(PIECES_PER_GROUP + i)
-        waiting = [project_output(piece) for piece in turn[:ahead]]
+        y_first = project_output(0)
         terms_1 = pooling_weights(1)
         repeat_weights(0, terms_0)
         repeat_weights(1, terms_1)
-        for k, piece in enumerate(turn):
-            pool(piece, waiting[k])
-            if k + ahead < len(turn):
-                waiting.append(project_output(turn[k + ahead]))
+        pool(0, y_first)
+        for piece in range(1, GROUPS * PIECES_PER_GROUP):
+            pool(piece, project_output(piece))
 
         result = held.tile([P, SENTENCES], F32, name="result")
         nc.scalar.activation(result[:], pooled[:], ACT.Tanh, bias=bm_column[:, 0:1], scale=1.0)

@@ -18,7 +18,7 @@ PER_PIECE = PIECE // T
 GROUP = 32
 GROUPS = SENTENCES // GROUP
 PIECES_PER_GROUP = GROUP // PER_PIECE
-VECTOR_SUMS = 5
+VECTOR_SUMS = 4
 
 FLOPS = 2 * P * (2 * P) * ENTRIES + 2 * P * ENTRIES
 
@@ -173,16 +173,24 @@ def tile_cabasc_kernel(tc, table, w, b1, w2, bm, offs, out):
                 product[:], coef[:, piece * PIECE : (piece + 1) * PIECE], 1.0 / T, y_mlp[:], ALU.add, ALU.mult
             )
             first = piece * PER_PIECE
+            last = piece == GROUPS * PIECES_PER_GROUP - 1
+            vector_sums = VECTOR_SUMS + 1 if last else VECTOR_SUMS
+            addends = product[:].rearrange("p (n t) -> p n t", t=T)
             nc.vector.tensor_reduce(
-                pooled[:, first : first + VECTOR_SUMS],
-                product[:, 0 : VECTOR_SUMS * T].rearrange("p (n t) -> p n t", t=T),
-                AXIS.X,
-                ALU.add,
+                pooled[:, first : first + vector_sums], addends[:, 0:vector_sums, :], AXIS.X, ALU.add
             )
-            for n in range(VECTOR_SUMS, PER_PIECE):
-                copied = work.tile([P, T], F32, name="copied")
+            others = addends[:, vector_sums:PER_PIECE, :]
+            if not last:
+                folded = work.tile([P, PER_PIECE - VECTOR_SUMS, T // 2], F32, name="folded")
+                nc.gpsimd.tensor_tensor(folded[:], others[:, :, 0 : T // 2], others[:, :, T // 2 : T], ALU.add)
+                others = folded[:]
+            for n in range(PER_PIECE - vector_sums):
+                copied = work.tile([P, 1, T], F32, name="copied")
                 nc.scalar.activation(
-                    copied[:], product[:, n * T : (n + 1) * T], ACT.Copy, accum_out=pooled[:, first + n : first + n + 1]
+                    copied[:, :, 0 : others.shape[2]],
+                    others[:, n : n + 1, :],
+                    ACT.Copy,
+                    accum_out=pooled[:, first + vector_sums + n : first + vector_sums + n + 1],
                 )
 
         for i in range(PIECES_PER_GROUP):

@@ -173,14 +173,14 @@ def tile_cabasc_kernel(tc, table, w, b1, w2, bm, offs, out):
                 product[:], coef[:, piece * PIECE : (piece + 1) * PIECE], 1.0 / T, y_mlp[:], ALU.add, ALU.mult
             )
             first = piece * PER_PIECE
-            last = piece == GROUPS * PIECES_PER_GROUP - 1
-            vector_sums = VECTOR_SUMS + 1 if last else VECTOR_SUMS
+            fold = piece < GROUPS * PIECES_PER_GROUP - 2
+            vector_sums = VECTOR_SUMS if fold else VECTOR_SUMS + 1
             addends = product[:].rearrange("p (n t) -> p n t", t=T)
             nc.vector.tensor_reduce(
                 pooled[:, first : first + vector_sums], addends[:, 0:vector_sums, :], AXIS.X, ALU.add
             )
             others = addends[:, vector_sums:PER_PIECE, :]
-            if not last:
+            if fold:
                 folded = work.tile([P, PER_PIECE - VECTOR_SUMS, T // 2], F32, name="folded")
                 nc.gpsimd.tensor_tensor(folded[:], others[:, :, 0 : T // 2], others[:, :, T // 2 : T], ALU.add)
                 others = folded[:]

import concourse.mybir as mybir

F32 = mybir.dt.float32
BF16 = mybir.dt.bfloat16
U16 = mybir.dt.uint16
I32 = mybir.dt.int32
ALU = mybir.AluOpType
ACT = mybir.ActivationFunctionType
AXIS = mybir.AxisListType

P = 128
WORDS = 2048
ENTRIES = 4096
T = 64
SENTENCES = ENTRIES // T
PIECE = 512
PER_PIECE = PIECE // T
GROUP = 32
GROUPS = SENTENCES // GROUP
PIECES_PER_GROUP = GROUP // PER_PIECE
VECTOR_SUMS = 4

FLOPS = 2 * P * (2 * P) * ENTRIES + 2 * P * ENTRIES


def tile_cabasc_kernel(tc, table, w, b1, w2, bm, offs, out):
    nc = tc.nc
    with (
        tc.tile_pool(name="held", bufs=1) as held,
        tc.tile_pool(name="work", bufs=6) as work,
        tc.tile_pool(name="small", bufs=2) as small,
        tc.psum_pool(name="psum", bufs=1) as psum,
    ):
        window = held.tile([P, WORDS], BF16, name="window")
        nc.scalar.dma_start(window[:], table)
        offsets = held.tile([P, ENTRIES // 16], U16, name="offsets")
        nc.sync.dma_start(offsets[:], offs)
        weights = held.tile([P, 2 * P], BF16, name="weights")
        nc.sync.dma_start(weights[:], w)
        b1_column = held.tile([P, 1], F32, name="b1_column")
        nc.sync.dma_start(b1_column[:], b1)
        w2_column = held.tile([P, 1], BF16, name="w2_column")
        nc.sync.dma_start(w2_column[:], w2)
        bm_column = held.tile([P, 1], F32, name="bm_column")
        nc.sync.dma_start(bm_column[:], bm)

        scratch = held.tile([P, 1], F32, name="scratch")
        nc.vector.memset(scratch[:], 0.0)
        nc.scalar.activation(scratch[:], scratch[:], ACT.Tanh)

        position = held.tile([P, PIECE], I32, name="position")
        nc.gpsimd.iota(position[:], pattern=[[0, PER_PIECE], [1, T]], base=0, channel_multiplier=0)
        dec = held.tile([P, PIECE], F32, name="dec")
        nc.vector.tensor_scalar(dec[:], position[:], -1.0 / T, 1.0, ALU.mult, ALU.add)

        w2_spread = held.tile([P, P + GROUP], BF16, name="w2_spread")
        nc.vector.memset(w2_spread[:], 0.0)
        nc.vector.tensor_copy(
            w2_spread[:].rearrange("p (c s) -> p c s", s=GROUP)[:, :, GROUP - 1 : GROUP],
            w2_column[:, 0:1].unsqueeze(2).to_broadcast([P, (P + GROUP) // GROUP, 1]),
        )

        pick = held.tile([P, GROUP], BF16, name="pick")
        nc.gpsimd.memset(pick[:], 0.0)
        for copy in range(3):
            nc.gpsimd.affine_select(
                out=pick[:],
                in_=pick[:],
                compare_op=ALU.not_equal,
                fill=1.0,
                base=-copy * GROUP,
                pattern=[[-1, GROUP]],
                channel_multiplier=1,
            )

        from_copy_1 = held.tile([P, 1], F32, name="from_copy_1")
        nc.vector.memset(from_copy_1[:], -1.0)
        nc.vector.memset(from_copy_1[0:GROUP], 0.0)
        from_copy_2 = held.tile([P, 1], F32, name="from_copy_2")
        nc.vector.memset(from_copy_2[:], -1.0)
        nc.vector.memset(from_copy_2[0 : 2 * GROUP], 0.0)

        hidden = held.tile([P, ENTRIES], BF16, name="hidden")
        coef = held.tile([P, ENTRIES], F32, name="coef")
        pooled = held.tile([P, SENTENCES], F32, name="pooled")

        def upper_half(tile):
            return tile[:].bitcast(BF16)[:, 1::2]

        def looked_up(piece):
            return window[:].indirect(offsets[:, piece * (PIECE // 16) : (piece + 1) * (PIECE // 16)])

        def attention_hidden(piece):
            y_att = psum.tile([P, PIECE], F32, name="y_att", tag="y", bufs=3)
            nc.tensor.matmul(y_att[:], weights[:, 0:P], looked_up(piece), start=True, stop=True)
            weighted = work.tile([P, PIECE], F32, name="weighted")
            nc.vector.tensor_tensor(weighted[:], y_att[:], dec[:], ALU.mult)
            nc.scalar.activation(
                hidden[:, piece * PIECE : (piece + 1) * PIECE],
                weighted[:],
                ACT.Tanh,
                bias=b1_column[:, 0:1],
                scale=1.0,
            )

        def pooling_weights(group):
            score = psum.tile([P, T], F32, name="score")
            for s in reversed(range(GROUP)):
                first = (group * GROUP + s) * T
                nc.tensor.matmul(
                    score[:],
                    w2_spread[:, GROUP - 1 - s : GROUP - 1 - s + P],
                    hidden[:, first : first + T],
                    start=(s == GROUP - 1),
                    stop=(s == 0),
                )
            neg_max = small.tile([P, 1], F32, name="neg_max")
            nc.vector.tensor_reduce(neg_max[:], score[:], AXIS.X, ALU.max, negate=True)
            expd = small.tile([P, T], F32, name="expd")
            exp_sum = small.tile([P, 1], F32, name="exp_sum")
            nc.scalar.activation(
                expd[:], score[:], ACT.Exp, bias=neg_max[:, 0:1], scale=1.0, accum_out=exp_sum[:, 0:1]
            )
            inverse = small.tile([P, 1], F32, name="inverse")
            nc.vector.reciprocal(inverse[:], exp_sum[:])
            value = small.tile([P, T], F32, name="value")
            nc.vector.scalar_tensor_tensor(
                value[:], expd[:], inverse[:, 0:1], dec[:, 0:T], ALU.mult, ALU.mult
            )
            rest = small.tile([P, T], F32, name="rest")
            nc.vector.scalar_tensor_tensor(
                rest[:], upper_half(value), from_copy_1[:, 0:1], value[:], ALU.mult, ALU.add
            )
            terms = small.tile([P, T], F32, name="terms")
            nc.vector.scalar_tensor_tensor(
                terms[:], upper_half(rest), from_copy_2[:, 0:1], rest[:], ALU.mult, ALU.add
            )
            return upper_half(terms)

        def repeat_weights(group, terms):
            repeated = []
            for i in range(PIECES_PER_GROUP):
                in_y_ring = group == 0 and i < 2
                bank = psum.tile(
                    [P, PIECE], F32, name=f"repeated{i}", tag="y" if in_y_ring else "repeated", bufs=3 if in_y_ring else 4
                )
                repeated.append(bank)
            for i in range(PIECES_PER_GROUP):
                for n in range(PER_PIECE):
                    s = i * PER_PIECE + n
                    nc.tensor.matmul(
                        repeated[i][:, n * T : (n + 1) * T],
                        pick[:, s : s + 1].to_broadcast([P, P]),
                        terms,
                        start=True,
                        stop=True,
                    )
            for i in range(PIECES_PER_GROUP):
                first = (group * PIECES_PER_GROUP + i) * PIECE
                nc.scalar.copy(coef[:, first : first + PIECE], repeated[i][:])

        def project_output(piece):
            in_score_bank = piece == 1
            y_mlp = psum.tile(
                [P, PIECE], F32, name="y_mlp", tag="score" if in_score_bank else "y", bufs=1 if in_score_bank else 3
            )
            nc.tensor.matmul(y_mlp[:], weights[:, P : 2 * P], looked_up(piece), start=True, stop=True)
            return y_mlp

        def pool(piece, y_mlp):
            product = work.tile([P, PIECE], F32, name="product")
            nc.vector.scalar_tensor_tensor(
                product[:], coef[:, piece * PIECE : (piece + 1) * PIECE], 1.0 / T, y_mlp[:], ALU.add, ALU.mult
            )
            first = piece * PER_PIECE
            fold = piece < GROUPS * PIECES_PER_GROUP - 2
            vector_sums = VECTOR_SUMS if fold else VECTOR_SUMS + 1
            addends = product[:].rearrange("p (n t) -> p n t", t=T)
            nc.vector.tensor_reduce(
                pooled[:, first : first + vector_sums], addends[:, 0:vector_sums, :], AXIS.X, ALU.add
            )
            others = addends[:, vector_sums:PER_PIECE, :]
            if fold:
                folded = work.tile([P, PER_PIECE - VECTOR_SUMS, T // 2], F32, name="folded")
                nc.gpsimd.tensor_tensor(folded[:], others[:, :, 0 : T // 2], others[:, :, T // 2 : T], ALU.add)
                others = folded[:]
            for n in range(PER_PIECE - vector_sums):
                copied = work.tile([P, 1, T], F32, name="copied")
                nc.scalar.activation(
                    copied[:, :, 0 : others.shape[2]],
                    others[:, n : n + 1, :],
                    ACT.Copy,
                    accum_out=pooled[:, first + vector_sums + n : first + vector_sums + n + 1],
                )

        for i in range(PIECES_PER_GROUP):
            attention_hidden(i)
        terms_0 = pooling_weights(0)
        for i in range(PIECES_PER_GROUP):
            attention_hidden(PIECES_PER_GROUP + i)
        y_first = project_output(0)
        terms_1 = pooling_weights(1)
        repeat_weights(0, terms_0)
        repeat_weights(1, terms_1)
        pool(0, y_first)
        for piece in range(1, GROUPS * PIECES_PER_GROUP):
            pool(piece, project_output(piece))

        result = held.tile([P, SENTENCES], F32, name="result")
        nc.scalar.activation(result[:], pooled[:], ACT.Tanh, bias=bm_column[:, 0:1], scale=1.0)
        nc.scalar.dma_start(out, result[:])
